import numpy as np
import ml_dtypes


def mxq(x, axis, fmt="e4m3"):
    dtype, down = {"e4m3": (ml_dtypes.float8_e4m3fn, 7), "e5m2": (ml_dtypes.float8_e5m2, 14)}[fmt]
    v = np.moveaxis(np.asarray(x, np.float32).astype(ml_dtypes.bfloat16).astype(np.float64), axis, -1)
    blocks = v.reshape(v.shape[:-1] + (-1, 32))
    amax = np.abs(blocks).max(-1, keepdims=True)
    byte = np.maximum(np.where(amax > 0, np.frexp(amax)[1] - 1 + 127, 0) - down, 1)
    scale = np.exp2(byte - 127.0)
    codes = (blocks / scale).astype(np.float32).astype(dtype).astype(np.float64)
    return np.moveaxis((codes * scale).reshape(v.shape), -1, axis)


WIDE = False


def mx_kscale(k):
    if not WIDE:
        return np.ones(k)
    levels = np.array([10, -10, 5, -5, 0])
    a = np.random.permutation(np.resize(levels, k // 512 * 4)).reshape(k // 512, 4)
    idx = np.arange(k)
    return np.exp2(a[idx // 512, idx % 128 // 32])


BF16 = ml_dtypes.bfloat16


def bf(x):
    return np.asarray(x, np.float32).astype(BF16)


def f64(x):
    return np.asarray(x).astype(np.float64)


E2M1 = np.array([0.0, 0.5, 1.0, 1.5, 2.0, 3.0, 4.0, 6.0, -0.0, -0.5, -1.0, -1.5, -2.0, -3.0, -4.0, -6.0])


def pack_weight(w, fmt):
    k, n = w.shape
    w = f64(bf(w)).reshape(k // 32, 32, n)
    amax = np.abs(w).max(1)
    if fmt == "e4m3":
        byte = np.frexp(amax)[1] - 1 + 127 - 7
    else:
        mant, ex = np.frexp(amax / 6.0)
        byte = np.where(mant > 0.5, ex, ex - 1) + 127
    byte = np.clip(np.where(amax > 0, byte, 1), 1, 254)
    scaled = (w * np.exp2(127.0 - byte)[:, None, :]).reshape(k, n).astype(np.float32)
    by_word = np.ascontiguousarray(scaled.reshape(k // 512, 128, 4, n).transpose(0, 1, 3, 2))
    if fmt == "e4m3":
        words = by_word.astype(ml_dtypes.float8_e4m3fn).view(np.uint8)
    else:
        c = by_word.astype(ml_dtypes.float4_e2m1fn).view(np.uint8) & 0xF
        words = c[..., 0::2] | (c[..., 1::2] << 4)
    return np.ascontiguousarray(words), np.ascontiguousarray(byte.astype(np.uint8).reshape(k // 512, 16, n))


def unpack_weight(words, scales, fmt):
    g, p, n, _ = words.shape
    if fmt == "e4m3":
        vals = np.ascontiguousarray(words).view(ml_dtypes.float8_e4m3fn).astype(np.float64)
    else:
        nib = np.empty((g, p, n, 4), np.uint8)
        nib[..., 0::2] = words & 0xF
        nib[..., 1::2] = words >> 4
        vals = E2M1[nib]
    vals = vals * np.repeat(np.exp2(scales.astype(np.float64) - 127.0), 8, axis=1)[..., None]
    return vals.transpose(0, 1, 3, 2).reshape(g * 512, n)

def pack4(w):
    words, scales = pack_weight(w, "e2m1")
    return words.reshape(words.shape[0], 128, -1), scales


def unpack4(words, scales):
    return unpack_weight(words.reshape(words.shape[0], 128, -1, 2), scales, "e2m1")


B, I, O = 128, 2048, 1024
DEGREE = 3
KNOTS = (0.2, 0.4, 0.6, 0.8)
SDIM = DEGREE + 1 + len(KNOTS)
T_MAX = 2.0


def truncated_power_basis(t):
    cols = [np.ones_like(t)]
    for p in range(1, DEGREE + 1):
        cols.append(t ** p)
    for c in KNOTS:
        cols.append(np.maximum(t - c, 0.0) ** DEGREE)
    return np.stack(cols, axis=1)


def setup_inputs():
    s = mx_kscale(I)
    t = np.random.random((B, 1)) * T_MAX
    x = np.random.random((B, I)) * s
    w = np.random.standard_normal((SDIM, I, O)) * (0.52 / np.sqrt(I)) / s[None, :, None]
    words, scales = pack4(w.reshape(-1, O))
    return {"inputs": bf(np.concatenate([t, x], axis=1)), "W_wts_words": words, "W_wts_scales": scales,
            "b_wts": bf(np.random.standard_normal((SDIM, O)) * 0.3)}


def reference(inputs, W_wts_words, W_wts_scales, b_wts):
    inputs = f64(inputs)
    treatment = inputs[:, 0]
    features = inputs[:, 1:]
    basis = truncated_power_basis(treatment)
    Wk = unpack4(W_wts_words, W_wts_scales).reshape(SDIM, I, O)
    P = mxq(features, 1, "e4m3") @ Wk
    out = (basis.T[:, :, None] * P).sum(0)
    out = out + (basis[:, :, None] * f64(b_wts)[None, :, :]).sum(1)
    return out

@@ -1,0 +1,160 @@
+from contextlib import ExitStack
+
+import concourse.mybir as mybir
+from concourse.masks import make_identity
+
+F32 = mybir.dt.float32
+BF16 = mybir.dt.bfloat16
+I32 = mybir.dt.int32
+U32 = mybir.dt.uint32
+U8 = mybir.dt.uint8
+FP8X4 = mybir.dt.float8_e4m3fn_x4
+FP4X4 = mybir.dt.float4_e2m1fn_x4
+ALU = mybir.AluOpType
+
+P = 128
+FEATURES = 2048
+OUTPUTS = 1024
+KNOTS = (0.2, 0.4, 0.6, 0.8)
+SDIM = 4 + len(KNOTS)
+
+PACK = 4
+K_PASS = P * PACK
+PASSES = FEATURES // K_PASS
+GROUPS = SDIM * PASSES
+N_TILE = 512
+N_TILES = OUTPUTS // N_TILE
+WORD_BYTES = 2
+
+RUNS = 2
+RUN_GROUPS = GROUPS // RUNS
+DMA_GROUPS = 8
+
+FLOPS = 2 * P * FEATURES * OUTPUTS * SDIM
+
+
+def tile_vclinear_w_e_kernel(tc, inputs, W_wts_words, W_wts_scales, b_wts, out):
+    nc = tc.nc
+    with ExitStack() as ctx:
+        ctx.enter_context(tc.manual_schedule())
+        keep = ctx.enter_context(tc.tile_pool(name="keep", bufs=1))
+        psum = ctx.enter_context(tc.psum_pool(name="psum", bufs=8))
+
+        words = []
+        planes = []
+
+        def load_weights(run):
+            first = run * RUN_GROUPS
+            plane = keep.tile([P, RUN_GROUPS, OUTPUTS], U8, name="plane%d" % run, align_bytes=64)
+            nc.vector.memset(plane[:].rearrange("p g n -> p (g n)").bitcast(I32), 0)
+            planes.append(plane)
+            for lo in range(0, RUN_GROUPS, DMA_GROUPS):
+                for j in range(2):
+                    for r in range(4):
+                        rows = W_wts_scales[first + lo : first + lo + DMA_GROUPS, 4 * j + r : 16 : 8, :]
+                        nc.sync.dma_start(
+                            out=plane[32 * j + r : P : 64, lo : lo + DMA_GROUPS, :].bitcast(I32),
+                            in_=rows.rearrange("g q n -> q g n").bitcast(I32),
+                        )
+            for g in range(first, first + RUN_GROUPS):
+                w = keep.tile([P, WORD_BYTES * OUTPUTS], U8, name="words%d" % g, align_bytes=64)
+                nc.sync.dma_start(out=w[:].bitcast(I32), in_=W_wts_words[g].bitcast(I32))
+                words.append(w)
+
+        x_in = keep.tile([P, 2 + FEATURES], BF16, align_bytes=64)
+        nc.sync.dma_start(out=x_in[:, 1 : 2 + FEATURES], in_=inputs[:, :])
+        b_rows = keep.tile([SDIM, OUTPUTS], BF16)
+        nc.scalar.dma_start(out=b_rows[:], in_=b_wts[:, :])
+        load_weights(0)
+
+        ident = keep.tile([P, P], F32)
+        make_identity(nc, ident[:])
+        b_f32 = keep.tile([P, OUTPUTS], F32)
+        nc.vector.memset(b_f32[:], 0.0)
+        basis = keep.tile([P, P], F32)
+        nc.vector.memset(basis[:], 0.0)
+        nc.scalar.copy(out=b_f32[0:SDIM, :], in_=b_rows[:])
+
+        t = basis[:, 1:2]
+        hinge = keep.tile([P, len(KNOTS)], F32)
+        hinge_sq = keep.tile([P, len(KNOTS)], F32)
+        nc.vector.memset(basis[:, 0:1], 1.0)
+        nc.vector.tensor_copy(out=t, in_=x_in[:, 1:2])
+        nc.vector.tensor_mul(basis[:, 2:3], t, t)
+        nc.vector.tensor_mul(basis[:, 3:4], basis[:, 2:3], t)
+        for j, knot in enumerate(KNOTS):
+            nc.vector.tensor_scalar(
+                out=hinge[:, j : j + 1], in0=t, scalar1=knot, scalar2=0.0, op0=ALU.subtract, op1=ALU.max
+            )
+        nc.vector.tensor_mul(hinge_sq[:], hinge[:], hinge[:])
+        nc.vector.tensor_mul(basis[:, 4:SDIM], hinge_sq[:], hinge[:])
+
+        x_words = x_in[:].bitcast(F32)
+        grouped = keep.tile([P, PASSES, P, PACK], BF16, align_bytes=64)
+        grouped_words = (
+            grouped[:]
+            .rearrange("p c b t -> p (c b t)")
+            .bitcast(F32)
+            .rearrange("p (c b u) -> p c b u", c=PASSES, u=2)
+        )
+        for c0 in range(0, PASSES, 2):
+            xt = psum.tile([P, 2, 2, P], F32, tag="bank")
+            for c in range(c0, c0 + 2):
+                for u in range(2):
+                    nc.tensor.transpose(
+                        xt[:, c - c0, u, :],
+                        x_words[:, 1 + 256 * c + u : 1 + 256 * (c + 1) : 2],
+                        ident[:],
+                    )
+            nc.scalar.copy(out=grouped_words[:, c0 : c0 + 2, :, :], in_=xt[:].rearrange("p c u b -> p c b u"))
+        x_codes = keep.tile([P, PASSES * P], U32, align_bytes=64)
+        x_scales = keep.tile([P, PASSES * P], U8, align_bytes=64)
+        nc.vector.quantize_mx(
+            out=x_codes[:].bitcast(FP8X4),
+            scales=x_scales[:],
+            in_=grouped[:].rearrange("p c b t -> p (c b t)"),
+        )
+
+        for run in range(1, RUNS):
+            load_weights(run)
+
+        basis_t_ps = psum.tile([P, P], F32, tag="bank")
+        nc.tensor.transpose(basis_t_ps[:], basis[:], ident[:])
+        basis_t = keep.tile([P, P], F32)
+        nc.scalar.copy(out=basis_t[:], in_=basis_t_ps[:])
+        acc = keep.tile([P, OUTPUTS], F32)
+        for n in range(N_TILES):
+            cols = slice(n * N_TILE, (n + 1) * N_TILE)
+            bias_ps = psum.tile([P, N_TILE], F32, tag="bank")
+            nc.tensor.matmul(out=bias_ps[:], lhsT=basis_t[:], rhs=b_f32[:, cols], start=True, stop=True)
+            nc.scalar.copy(out=acc[:, cols], in_=bias_ps[:])
+
+        for s in range(SDIM):
+            product = [psum.tile([P, N_TILE], F32, tag="bank", name="product%d" % n) for n in range(N_TILES)]
+            for c in range(PASSES):
+                g = PASSES * s + c
+                plane = planes[g // RUN_GROUPS]
+                for n in range(N_TILES):
+                    nc.tensor.matmul_mx(
+                        out=product[n][:],
+                        lhsT=x_codes[:, c * P : (c + 1) * P].bitcast(FP8X4),
+                        lhsT_scale=x_scales[:, c * P : (c + 1) * P],
+                        rhs=words[g][:, n * N_TILE * WORD_BYTES : (n + 1) * N_TILE * WORD_BYTES].bitcast(FP4X4),
+                        rhs_scale=plane[:, g % RUN_GROUPS, n * N_TILE : (n + 1) * N_TILE],
+                        start=(c == 0),
+                        stop=(c == PASSES - 1),
+                    )
+            for n in range(N_TILES):
+                cols = slice(n * N_TILE, (n + 1) * N_TILE)
+                nc.vector.scalar_tensor_tensor(
+                    out=acc[:, cols],
+                    in0=product[n][:],
+                    scalar=basis[:, s : s + 1],
+                    in1=acc[:, cols],
+                    op0=ALU.mult,
+                    op1=ALU.add,
+                )
+
+        for n in range(N_TILES):
+            cols = slice(n * N_TILE, (n + 1) * N_TILE)
+            nc.sync.dma_start(out=out[:, cols], in_=acc[:, cols])

@@ -26,7 +26,7 @@ N_TILE = 512
 N_TILES = OUTPUTS // N_TILE
 WORD_BYTES = 2
 
-RUNS = 2
+RUNS = 1
 RUN_GROUPS = GROUPS // RUNS
 DMA_GROUPS = 8
 
@@ -40,32 +40,40 @@ def tile_vclinear_w_e_kernel(tc, inputs, W_wts_words, W_wts_scales, b_wts, out):
         keep = ctx.enter_context(tc.tile_pool(name="keep", bufs=1))
         psum = ctx.enter_context(tc.psum_pool(name="psum", bufs=8))
 
-        words = []
-        planes = []
-
-        def load_weights(run):
-            first = run * RUN_GROUPS
-            plane = keep.tile([P, RUN_GROUPS, OUTPUTS], U8, name="plane%d" % run, align_bytes=64)
-            nc.vector.memset(plane[:].rearrange("p g n -> p (g n)").bitcast(I32), 0)
-            planes.append(plane)
-            for lo in range(0, RUN_GROUPS, DMA_GROUPS):
-                for j in range(2):
-                    for r in range(4):
-                        rows = W_wts_scales[first + lo : first + lo + DMA_GROUPS, 4 * j + r : 16 : 8, :]
-                        nc.sync.dma_start(
-                            out=plane[32 * j + r : P : 64, lo : lo + DMA_GROUPS, :].bitcast(I32),
-                            in_=rows.rearrange("g q n -> q g n").bitcast(I32),
-                        )
-            for g in range(first, first + RUN_GROUPS):
-                w = keep.tile([P, WORD_BYTES * OUTPUTS], U8, name="words%d" % g, align_bytes=64)
-                nc.sync.dma_start(out=w[:].bitcast(I32), in_=W_wts_words[g].bitcast(I32))
-                words.append(w)
-
         x_in = keep.tile([P, 2 + FEATURES], BF16, align_bytes=64)
         nc.sync.dma_start(out=x_in[:, 1 : 2 + FEATURES], in_=inputs[:, :])
         b_rows = keep.tile([SDIM, OUTPUTS], BF16)
         nc.scalar.dma_start(out=b_rows[:], in_=b_wts[:, :])
-        load_weights(0)
+
+        words = [keep.tile([P, WORD_BYTES * OUTPUTS], U8, name="words%d" % g, align_bytes=64) for g in range(GROUPS)]
+        planes = [keep.tile([P, RUN_GROUPS, OUTPUTS], U8, name="planes%d" % run, align_bytes=64) for run in range(RUNS)]
+
+        def load_words(g, first_tile, n_tiles):
+            cols = slice(first_tile * N_TILE * WORD_BYTES, (first_tile + n_tiles) * N_TILE * WORD_BYTES)
+            nc.sync.dma_start(out=words[g][:, cols].bitcast(I32), in_=W_wts_words[g, :, cols].bitcast(I32))
+
+        def load_scales(run):
+            for lo in range(0, RUN_GROUPS, DMA_GROUPS):
+                part = planes[run][:, lo : lo + DMA_GROUPS, :]
+                nc.vector.memset(part.rearrange("p g n -> p (g n)").bitcast(I32), 0)
+                first = run * RUN_GROUPS + lo
+                for j in range(2):
+                    for r in range(4):
+                        rows = W_wts_scales[first : first + DMA_GROUPS, 4 * j + r : 16 : 8, :]
+                        nc.sync.dma_start(
+                            out=part[32 * j + r : P : 64, :, :].bitcast(I32),
+                            in_=rows.rearrange("g q n -> q g n").bitcast(I32),
+                        )
+
+        for g in range(PASSES):
+            load_words(g, 0, N_TILES)
+        for run in range(RUNS):
+            load_scales(run)
+            for g in range(max(run * RUN_GROUPS, PASSES), min((run + 1) * RUN_GROUPS, GROUPS - PASSES)):
+                load_words(g, 0, N_TILES)
+        for n in range(N_TILES):
+            for g in range(GROUPS - PASSES, GROUPS):
+                load_words(g, n, 1)
 
         ident = keep.tile([P, P], F32)
         make_identity(nc, ident[:])
@@ -115,9 +123,6 @@ def tile_vclinear_w_e_kernel(tc, inputs, W_wts_words, W_wts_scales, b_wts, out):
             in_=grouped[:].rearrange("p c b t -> p (c b t)"),
         )
 
-        for run in range(1, RUNS):
-            load_weights(run)
-
         basis_t_ps = psum.tile([P, P], F32, tag="bank")
         nc.tensor.transpose(basis_t_ps[:], basis[:], ident[:])
         basis_t = keep.tile([P, P], F32)
@@ -131,19 +136,21 @@ def tile_vclinear_w_e_kernel(tc, inputs, W_wts_words, W_wts_scales, b_wts, out):
 
         for s in range(SDIM):
             product = [psum.tile([P, N_TILE], F32, tag="bank", name="product%d" % n) for n in range(N_TILES)]
-            for c in range(PASSES):
+            if s < SDIM - 1:
+                order = [(c, n) for c in range(PASSES) for n in range(N_TILES)]
+            else:
+                order = [(c, n) for n in range(N_TILES) for c in range(PASSES)]
+            for c, n in order:
                 g = PASSES * s + c
-                plane = planes[g // RUN_GROUPS]
-                for n in range(N_TILES):
-                    nc.tensor.matmul_mx(
-                        out=product[n][:],
-                        lhsT=x_codes[:, c * P : (c + 1) * P].bitcast(FP8X4),
-                        lhsT_scale=x_scales[:, c * P : (c + 1) * P],
-                        rhs=words[g][:, n * N_TILE * WORD_BYTES : (n + 1) * N_TILE * WORD_BYTES].bitcast(FP4X4),
-                        rhs_scale=plane[:, g % RUN_GROUPS, n * N_TILE : (n + 1) * N_TILE],
-                        start=(c == 0),
-                        stop=(c == PASSES - 1),
-                    )
+                nc.tensor.matmul_mx(
+                    out=product[n][:],
+                    lhsT=x_codes[:, c * P : (c + 1) * P].bitcast(FP8X4),
+                    lhsT_scale=x_scales[:, c * P : (c + 1) * P],
+                    rhs=words[g][:, n * N_TILE * WORD_BYTES : (n + 1) * N_TILE * WORD_BYTES].bitcast(FP4X4),
+                    rhs_scale=planes[g // RUN_GROUPS][:, g % RUN_GROUPS, n * N_TILE : (n + 1) * N_TILE],
+                    start=(c == 0),
+                    stop=(c == PASSES - 1),
+                )
             for n in range(N_TILES):
                 cols = slice(n * N_TILE, (n + 1) * N_TILE)
                 nc.vector.scalar_tensor_tensor(
@@ -154,7 +161,5 @@ def tile_vclinear_w_e_kernel(tc, inputs, W_wts_words, W_wts_scales, b_wts, out):
                     op0=ALU.mult,
                     op1=ALU.add,
                 )
-
-        for n in range(N_TILES):
-            cols = slice(n * N_TILE, (n + 1) * N_TILE)
-            nc.sync.dma_start(out=out[:, cols], in_=acc[:, cols])
+                if s == SDIM - 1:
+                    nc.sync.dma_start(out=out[:, cols], in_=acc[:, cols])

@@ -40,8 +40,10 @@ def tile_vclinear_w_e_kernel(tc, inputs, W_wts_words, W_wts_scales, b_wts, out):
         keep = ctx.enter_context(tc.tile_pool(name="keep", bufs=1))
         psum = ctx.enter_context(tc.psum_pool(name="psum", bufs=8))
 
-        x_in = keep.tile([P, 2 + FEATURES], BF16, align_bytes=64)
-        nc.sync.dma_start(out=x_in[:, 1 : 2 + FEATURES], in_=inputs[:, :])
+        x_in = keep.tile([P, FEATURES], BF16, align_bytes=64)
+        nc.sync.dma_start(out=x_in[:], in_=inputs[:, 1 : 1 + FEATURES])
+        t_in = keep.tile([P, 2], BF16)
+        nc.scalar.dma_start(out=t_in[:], in_=inputs[:, 0:2])
         b_rows = keep.tile([SDIM, OUTPUTS], BF16)
         nc.scalar.dma_start(out=b_rows[:], in_=b_wts[:, :])
 
@@ -87,7 +89,7 @@ def tile_vclinear_w_e_kernel(tc, inputs, W_wts_words, W_wts_scales, b_wts, out):
         hinge = keep.tile([P, len(KNOTS)], F32)
         hinge_sq = keep.tile([P, len(KNOTS)], F32)
         nc.vector.memset(basis[:, 0:1], 1.0)
-        nc.vector.tensor_copy(out=t, in_=x_in[:, 1:2])
+        nc.vector.tensor_copy(out=t, in_=t_in[:, 0:1])
         nc.vector.tensor_mul(basis[:, 2:3], t, t)
         nc.vector.tensor_mul(basis[:, 3:4], basis[:, 2:3], t)
         for j, knot in enumerate(KNOTS):
@@ -111,7 +113,7 @@ def tile_vclinear_w_e_kernel(tc, inputs, W_wts_words, W_wts_scales, b_wts, out):
                 for u in range(2):
                     nc.tensor.transpose(
                         xt[:, c - c0, u, :],
-                        x_words[:, 1 + 256 * c + u : 1 + 256 * (c + 1) : 2],
+                        x_words[:, 256 * c + u : 256 * (c + 1) : 2],
                         ident[:],
                     )
             nc.scalar.copy(out=grouped_words[:, c0 : c0 + 2, :, :], in_=xt[:].rearrange("p c u b -> p c b u"))

@@ -41,63 +41,43 @@ def tile_vclinear_w_e_kernel(tc, inputs, W_wts_words, W_wts_scales, b_wts, out):
         psum = ctx.enter_context(tc.psum_pool(name="psum", bufs=8))
 
         x_in = keep.tile([P, FEATURES], BF16, align_bytes=64)
-        nc.sync.dma_start(out=x_in[:], in_=inputs[:, 1 : 1 + FEATURES])
         t_in = keep.tile([P, 2], BF16)
-        nc.scalar.dma_start(out=t_in[:], in_=inputs[:, 0:2])
         b_rows = keep.tile([SDIM, OUTPUTS], BF16)
-        nc.scalar.dma_start(out=b_rows[:], in_=b_wts[:, :])
-
         words = [keep.tile([P, WORD_BYTES * OUTPUTS], U8, name="words%d" % g, align_bytes=64) for g in range(GROUPS)]
-        planes = [keep.tile([P, RUN_GROUPS, OUTPUTS], U8, name="planes%d" % run, align_bytes=64) for run in range(RUNS)]
+        planes = keep.tile([P, GROUPS, OUTPUTS], U8, align_bytes=64)
 
         def load_words(g, first_tile, n_tiles):
             cols = slice(first_tile * N_TILE * WORD_BYTES, (first_tile + n_tiles) * N_TILE * WORD_BYTES)
             nc.sync.dma_start(out=words[g][:, cols].bitcast(I32), in_=W_wts_words[g, :, cols].bitcast(I32))
 
-        def load_scales(run):
-            for lo in range(0, RUN_GROUPS, DMA_GROUPS):
-                part = planes[run][:, lo : lo + DMA_GROUPS, :]
-                nc.vector.memset(part.rearrange("p g n -> p (g n)").bitcast(I32), 0)
-                first = run * RUN_GROUPS + lo
-                for j in range(2):
-                    for r in range(4):
-                        rows = W_wts_scales[first : first + DMA_GROUPS, 4 * j + r : 16 : 8, :]
-                        nc.sync.dma_start(
-                            out=part[32 * j + r : P : 64, :, :].bitcast(I32),
-                            in_=rows.rearrange("g q n -> q g n").bitcast(I32),
-                        )
+        def zero_planes(lo):
+            part = planes[:, lo : lo + DMA_GROUPS, :]
+            nc.vector.memset(part.rearrange("p g n -> p (g n)").bitcast(I32), 0)
 
+        def load_scales(lo):
+            part = planes[:, lo : lo + DMA_GROUPS, :]
+            for j in range(2):
+                for r in range(4):
+                    rows = W_wts_scales[lo : lo + DMA_GROUPS, 4 * j + r : 16 : 8, :]
+                    nc.sync.dma_start(
+                        out=part[32 * j + r : P : 64, :, :].bitcast(I32),
+                        in_=rows.rearrange("g q n -> q g n").bitcast(I32),
+                    )
+
+        nc.sync.dma_start(out=x_in[:], in_=inputs[:, 1 : 1 + FEATURES])
+        nc.scalar.dma_start(out=t_in[:], in_=inputs[:, 0:2])
+        nc.scalar.dma_start(out=b_rows[:], in_=b_wts[:, :])
         for g in range(PASSES):
             load_words(g, 0, N_TILES)
-        for run in range(RUNS):
-            load_scales(run)
-            for g in range(max(run * RUN_GROUPS, PASSES), min((run + 1) * RUN_GROUPS, GROUPS - PASSES)):
-                load_words(g, 0, N_TILES)
-        for n in range(N_TILES):
-            for g in range(GROUPS - PASSES, GROUPS):
-                load_words(g, n, 1)
-
+        warm = keep.tile([P, 2], F32)
+        nc.vector.memset(warm[:, 0:1], 0.0)
+        nc.scalar.copy(out=warm[:, 1:2], in_=warm[:, 0:1])
         ident = keep.tile([P, P], F32)
         make_identity(nc, ident[:])
-        b_f32 = keep.tile([P, OUTPUTS], F32)
-        nc.vector.memset(b_f32[:], 0.0)
-        basis = keep.tile([P, P], F32)
-        nc.vector.memset(basis[:], 0.0)
-        nc.scalar.copy(out=b_f32[0:SDIM, :], in_=b_rows[:])
-
-        t = basis[:, 1:2]
-        hinge = keep.tile([P, len(KNOTS)], F32)
-        hinge_sq = keep.tile([P, len(KNOTS)], F32)
-        nc.vector.memset(basis[:, 0:1], 1.0)
-        nc.vector.tensor_copy(out=t, in_=t_in[:, 0:1])
-        nc.vector.tensor_mul(basis[:, 2:3], t, t)
-        nc.vector.tensor_mul(basis[:, 3:4], basis[:, 2:3], t)
-        for j, knot in enumerate(KNOTS):
-            nc.vector.tensor_scalar(
-                out=hinge[:, j : j + 1], in0=t, scalar1=knot, scalar2=0.0, op0=ALU.subtract, op1=ALU.max
-            )
-        nc.vector.tensor_mul(hinge_sq[:], hinge[:], hinge[:])
-        nc.vector.tensor_mul(basis[:, 4:SDIM], hinge_sq[:], hinge[:])
+        zero_planes(0)
+        zero_planes(DMA_GROUPS)
+        load_scales(0)
+        load_scales(DMA_GROUPS)
 
         x_words = x_in[:].bitcast(F32)
         grouped = keep.tile([P, PASSES, P, PACK], BF16, align_bytes=64)
@@ -125,16 +105,46 @@ def tile_vclinear_w_e_kernel(tc, inputs, W_wts_words, W_wts_scales, b_wts, out):
             in_=grouped[:].rearrange("p c b t -> p (c b t)"),
         )
 
-        basis_t_ps = psum.tile([P, P], F32, tag="bank")
-        nc.tensor.transpose(basis_t_ps[:], basis[:], ident[:])
-        basis_t = keep.tile([P, P], F32)
-        nc.scalar.copy(out=basis_t[:], in_=basis_t_ps[:])
-        acc = keep.tile([P, OUTPUTS], F32)
+        for lo in range(2 * DMA_GROUPS, GROUPS, DMA_GROUPS):
+            zero_planes(lo)
+            load_scales(lo)
+        for g in range(PASSES, GROUPS - PASSES):
+            load_words(g, 0, N_TILES)
         for n in range(N_TILES):
-            cols = slice(n * N_TILE, (n + 1) * N_TILE)
-            bias_ps = psum.tile([P, N_TILE], F32, tag="bank")
-            nc.tensor.matmul(out=bias_ps[:], lhsT=basis_t[:], rhs=b_f32[:, cols], start=True, stop=True)
-            nc.scalar.copy(out=acc[:, cols], in_=bias_ps[:])
+            for g in range(GROUPS - PASSES, GROUPS):
+                load_words(g, n, 1)
+
+        b_f32 = keep.tile([P, OUTPUTS], F32)
+        nc.vector.memset(b_f32[:], 0.0)
+        basis = keep.tile([P, P], F32)
+        nc.vector.memset(basis[:], 0.0)
+        nc.scalar.copy(out=b_f32[0:SDIM, :], in_=b_rows[:])
+        t = basis[:, 1:2]
+        hinge = keep.tile([P, len(KNOTS)], F32)
+        hinge_sq = keep.tile([P, len(KNOTS)], F32)
+        nc.vector.memset(basis[:, 0:1], 1.0)
+        nc.vector.tensor_copy(out=t, in_=t_in[:, 0:1])
+        nc.vector.tensor_mul(basis[:, 2:3], t, t)
+        nc.vector.tensor_mul(basis[:, 3:4], basis[:, 2:3], t)
+        for j, knot in enumerate(KNOTS):
+            nc.vector.tensor_scalar(
+                out=hinge[:, j : j + 1], in0=t, scalar1=knot, scalar2=0.0, op0=ALU.subtract, op1=ALU.max
+            )
+        nc.vector.tensor_mul(hinge_sq[:], hinge[:], hinge[:])
+        nc.vector.tensor_mul(basis[:, 4:SDIM], hinge_sq[:], hinge[:])
+
+        acc = keep.tile([P, OUTPUTS], F32)
+
+        def bias_product():
+            basis_t_ps = psum.tile([P, P], F32, tag="bank")
+            nc.tensor.transpose(basis_t_ps[:], basis[:], ident[:])
+            basis_t = keep.tile([P, P], F32)
+            nc.scalar.copy(out=basis_t[:], in_=basis_t_ps[:])
+            for n in range(N_TILES):
+                cols = slice(n * N_TILE, (n + 1) * N_TILE)
+                bias_ps = psum.tile([P, N_TILE], F32, tag="bank")
+                nc.tensor.matmul(out=bias_ps[:], lhsT=basis_t[:], rhs=b_f32[:, cols], start=True, stop=True)
+                nc.scalar.copy(out=acc[:, cols], in_=bias_ps[:])
 
         for s in range(SDIM):
             product = [psum.tile([P, N_TILE], F32, tag="bank", name="product%d" % n) for n in range(N_TILES)]
@@ -149,10 +159,12 @@ def tile_vclinear_w_e_kernel(tc, inputs, W_wts_words, W_wts_scales, b_wts, out):
                     lhsT=x_codes[:, c * P : (c + 1) * P].bitcast(FP8X4),
                     lhsT_scale=x_scales[:, c * P : (c + 1) * P],
                     rhs=words[g][:, n * N_TILE * WORD_BYTES : (n + 1) * N_TILE * WORD_BYTES].bitcast(FP4X4),
-                    rhs_scale=planes[g // RUN_GROUPS][:, g % RUN_GROUPS, n * N_TILE : (n + 1) * N_TILE],
+                    rhs_scale=planes[:, g, n * N_TILE : (n + 1) * N_TILE],
                     start=(c == 0),
                     stop=(c == PASSES - 1),
                 )
+            if s == 0:
+                bias_product()
             for n in range(N_TILES):
                 cols = slice(n * N_TILE, (n + 1) * N_TILE)
                 nc.vector.scalar_tensor_tensor(

@@ -44,18 +44,21 @@ def tile_vclinear_w_e_kernel(tc, inputs, W_wts_words, W_wts_scales, b_wts, out):
         t_in = keep.tile([P, 2], BF16)
         b_rows = keep.tile([SDIM, OUTPUTS], BF16)
         words = [keep.tile([P, WORD_BYTES * OUTPUTS], U8, name="words%d" % g, align_bytes=64) for g in range(GROUPS)]
-        planes = keep.tile([P, GROUPS, OUTPUTS], U8, align_bytes=64)
+        planes = [
+            keep.tile([P, DMA_GROUPS, OUTPUTS], U8, name="planes%d" % lo, align_bytes=64)
+            for lo in range(0, GROUPS, DMA_GROUPS)
+        ]
 
         def load_words(g, first_tile, n_tiles):
             cols = slice(first_tile * N_TILE * WORD_BYTES, (first_tile + n_tiles) * N_TILE * WORD_BYTES)
             nc.sync.dma_start(out=words[g][:, cols].bitcast(I32), in_=W_wts_words[g, :, cols].bitcast(I32))
 
         def zero_planes(lo):
-            part = planes[:, lo : lo + DMA_GROUPS, :]
+            part = planes[lo // DMA_GROUPS][:]
             nc.vector.memset(part.rearrange("p g n -> p (g n)").bitcast(I32), 0)
 
         def load_scales(lo):
-            part = planes[:, lo : lo + DMA_GROUPS, :]
+            part = planes[lo // DMA_GROUPS]
             for j in range(2):
                 for r in range(4):
                     rows = W_wts_scales[lo : lo + DMA_GROUPS, 4 * j + r : 16 : 8, :]
@@ -74,10 +77,28 @@ def tile_vclinear_w_e_kernel(tc, inputs, W_wts_words, W_wts_scales, b_wts, out):
         nc.scalar.copy(out=warm[:, 1:2], in_=warm[:, 0:1])
         ident = keep.tile([P, P], F32)
         make_identity(nc, ident[:])
+        b_f32 = keep.tile([P, OUTPUTS], F32)
+        nc.gpsimd.memset(b_f32[:], 0.0)
+        basis = keep.tile([P, P], F32)
+        nc.gpsimd.memset(basis[:], 0.0)
         zero_planes(0)
         zero_planes(DMA_GROUPS)
         load_scales(0)
         load_scales(DMA_GROUPS)
+
+        t = basis[:, 1:2]
+        hinge = keep.tile([P, len(KNOTS)], F32)
+        hinge_sq = keep.tile([P, len(KNOTS)], F32)
+        nc.vector.memset(basis[:, 0:1], 1.0)
+        nc.vector.tensor_copy(out=t, in_=t_in[:, 0:1])
+        nc.vector.tensor_mul(basis[:, 2:3], t, t)
+        nc.vector.tensor_mul(basis[:, 3:4], basis[:, 2:3], t)
+        for j, knot in enumerate(KNOTS):
+            nc.vector.tensor_scalar(
+                out=hinge[:, j : j + 1], in0=t, scalar1=knot, scalar2=0.0, op0=ALU.subtract, op1=ALU.max
+            )
+        nc.vector.tensor_mul(hinge_sq[:], hinge[:], hinge[:])
+        nc.vector.tensor_mul(basis[:, 4:SDIM], hinge_sq[:], hinge[:])
 
         x_words = x_in[:].bitcast(F32)
         grouped = keep.tile([P, PASSES, P, PACK], BF16, align_bytes=64)
@@ -97,6 +118,7 @@ def tile_vclinear_w_e_kernel(tc, inputs, W_wts_words, W_wts_scales, b_wts, out):
                         ident[:],
                     )
             nc.scalar.copy(out=grouped_words[:, c0 : c0 + 2, :, :], in_=xt[:].rearrange("p c u b -> p c b u"))
+        nc.scalar.copy(out=b_f32[0:SDIM, :], in_=b_rows[:])
         x_codes = keep.tile([P, PASSES * P], U32, align_bytes=64)
         x_scales = keep.tile([P, PASSES * P], U8, align_bytes=64)
         nc.vector.quantize_mx(
@@ -114,25 +136,6 @@ def tile_vclinear_w_e_kernel(tc, inputs, W_wts_words, W_wts_scales, b_wts, out):
             for g in range(GROUPS - PASSES, GROUPS):
                 load_words(g, n, 1)
 
-        b_f32 = keep.tile([P, OUTPUTS], F32)
-        nc.vector.memset(b_f32[:], 0.0)
-        basis = keep.tile([P, P], F32)
-        nc.vector.memset(basis[:], 0.0)
-        nc.scalar.copy(out=b_f32[0:SDIM, :], in_=b_rows[:])
-        t = basis[:, 1:2]
-        hinge = keep.tile([P, len(KNOTS)], F32)
-        hinge_sq = keep.tile([P, len(KNOTS)], F32)
-        nc.vector.memset(basis[:, 0:1], 1.0)
-        nc.vector.tensor_copy(out=t, in_=t_in[:, 0:1])
-        nc.vector.tensor_mul(basis[:, 2:3], t, t)
-        nc.vector.tensor_mul(basis[:, 3:4], basis[:, 2:3], t)
-        for j, knot in enumerate(KNOTS):
-            nc.vector.tensor_scalar(
-                out=hinge[:, j : j + 1], in0=t, scalar1=knot, scalar2=0.0, op0=ALU.subtract, op1=ALU.max
-            )
-        nc.vector.tensor_mul(hinge_sq[:], hinge[:], hinge[:])
-        nc.vector.tensor_mul(basis[:, 4:SDIM], hinge_sq[:], hinge[:])
-
         acc = keep.tile([P, OUTPUTS], F32)
 
         def bias_product():
@@ -145,6 +148,8 @@ def tile_vclinear_w_e_kernel(tc, inputs, W_wts_words, W_wts_scales, b_wts, out):
                 bias_ps = psum.tile([P, N_TILE], F32, tag="bank")
                 nc.tensor.matmul(out=bias_ps[:], lhsT=basis_t[:], rhs=b_f32[:, cols], start=True, stop=True)
                 nc.scalar.copy(out=acc[:, cols], in_=bias_ps[:])
+
+        bias_product()
 
         for s in range(SDIM):
             product = [psum.tile([P, N_TILE], F32, tag="bank", name="product%d" % n) for n in range(N_TILES)]
@@ -159,12 +164,10 @@ def tile_vclinear_w_e_kernel(tc, inputs, W_wts_words, W_wts_scales, b_wts, out):
                     lhsT=x_codes[:, c * P : (c + 1) * P].bitcast(FP8X4),
                     lhsT_scale=x_scales[:, c * P : (c + 1) * P],
                     rhs=words[g][:, n * N_TILE * WORD_BYTES : (n + 1) * N_TILE * WORD_BYTES].bitcast(FP4X4),
-                    rhs_scale=planes[:, g, n * N_TILE : (n + 1) * N_TILE],
+                    rhs_scale=planes[g // DMA_GROUPS][:, g % DMA_GROUPS, n * N_TILE : (n + 1) * N_TILE],
                     start=(c == 0),
                     stop=(c == PASSES - 1),
                 )
-            if s == 0:
-                bias_product()
             for n in range(N_TILES):
                 cols = slice(n * N_TILE, (n + 1) * N_TILE)
                 nc.vector.scalar_tensor_tensor(

@@ -43,15 +43,20 @@ def tile_vclinear_w_e_kernel(tc, inputs, W_wts_words, W_wts_scales, b_wts, out):
         x_in = keep.tile([P, FEATURES], BF16, align_bytes=64)
         t_in = keep.tile([P, 2], BF16)
         b_rows = keep.tile([SDIM, OUTPUTS], BF16)
-        words = [keep.tile([P, WORD_BYTES * OUTPUTS], U8, name="words%d" % g, align_bytes=64) for g in range(GROUPS)]
+        words = [
+            keep.tile([P, 2, WORD_BYTES * OUTPUTS], U8, name="words%d" % i, align_bytes=64) for i in range(GROUPS // 2)
+        ]
         planes = [
             keep.tile([P, DMA_GROUPS, OUTPUTS], U8, name="planes%d" % lo, align_bytes=64)
             for lo in range(0, GROUPS, DMA_GROUPS)
         ]
 
-        def load_words(g, first_tile, n_tiles):
+        def load_words(g, n_groups, first_tile, n_tiles):
             cols = slice(first_tile * N_TILE * WORD_BYTES, (first_tile + n_tiles) * N_TILE * WORD_BYTES)
-            nc.sync.dma_start(out=words[g][:, cols].bitcast(I32), in_=W_wts_words[g, :, cols].bitcast(I32))
+            nc.sync.dma_start(
+                out=words[g // 2][:, g % 2 : g % 2 + n_groups, cols].bitcast(I32),
+                in_=W_wts_words[g : g + n_groups, :, cols].rearrange("g p b -> p g b").bitcast(I32),
+            )
 
         def zero_planes(lo):
             part = planes[lo // DMA_GROUPS][:]
@@ -70,8 +75,8 @@ def tile_vclinear_w_e_kernel(tc, inputs, W_wts_words, W_wts_scales, b_wts, out):
         nc.sync.dma_start(out=x_in[:], in_=inputs[:, 1 : 1 + FEATURES])
         nc.scalar.dma_start(out=t_in[:], in_=inputs[:, 0:2])
         nc.scalar.dma_start(out=b_rows[:], in_=b_wts[:, :])
-        for g in range(PASSES):
-            load_words(g, 0, N_TILES)
+        for g in range(0, PASSES, 2):
+            load_words(g, 2, 0, N_TILES)
         warm = keep.tile([P, 2], F32)
         nc.vector.memset(warm[:, 0:1], 0.0)
         nc.scalar.copy(out=warm[:, 1:2], in_=warm[:, 0:1])
@@ -130,11 +135,12 @@ def tile_vclinear_w_e_kernel(tc, inputs, W_wts_words, W_wts_scales, b_wts, out):
         for lo in range(2 * DMA_GROUPS, GROUPS, DMA_GROUPS):
             zero_planes(lo)
             load_scales(lo)
-        for g in range(PASSES, GROUPS - PASSES):
-            load_words(g, 0, N_TILES)
-        for n in range(N_TILES):
-            for g in range(GROUPS - PASSES, GROUPS):
-                load_words(g, n, 1)
+        for g in range(PASSES, GROUPS - PASSES, 2):
+            load_words(g, 2, 0, N_TILES)
+        for g in range(GROUPS - PASSES, GROUPS, 2):
+            load_words(g, 2, 0, 1)
+        for g in range(GROUPS - PASSES, GROUPS):
+            load_words(g, 1, 1, 1)
 
         acc = keep.tile([P, OUTPUTS], F32)
 
@@ -163,7 +169,7 @@ def tile_vclinear_w_e_kernel(tc, inputs, W_wts_words, W_wts_scales, b_wts, out):
                     out=product[n][:],
                     lhsT=x_codes[:, c * P : (c + 1) * P].bitcast(FP8X4),
                     lhsT_scale=x_scales[:, c * P : (c + 1) * P],
-                    rhs=words[g][:, n * N_TILE * WORD_BYTES : (n + 1) * N_TILE * WORD_BYTES].bitcast(FP4X4),
+                    rhs=words[g // 2][:, g % 2, n * N_TILE * WORD_BYTES : (n + 1) * N_TILE * WORD_BYTES].bitcast(FP4X4),
                     rhs_scale=planes[g // DMA_GROUPS][:, g % DMA_GROUPS, n * N_TILE : (n + 1) * N_TILE],
                     start=(c == 0),
                     stop=(c == PASSES - 1),

@@ -29,6 +29,7 @@ WORD_BYTES = 2
 RUNS = 1
 RUN_GROUPS = GROUPS // RUNS
 DMA_GROUPS = 8
+AHEAD = 3
 
 FLOPS = 2 * P * FEATURES * OUTPUTS * SDIM
 
@@ -75,7 +76,7 @@ def tile_vclinear_w_e_kernel(tc, inputs, W_wts_words, W_wts_scales, b_wts, out):
         nc.sync.dma_start(out=x_in[:], in_=inputs[:, 1 : 1 + FEATURES])
         nc.scalar.dma_start(out=t_in[:], in_=inputs[:, 0:2])
         nc.scalar.dma_start(out=b_rows[:], in_=b_wts[:, :])
-        for g in range(0, PASSES, 2):
+        for g in range(0, AHEAD * PASSES, 2):
             load_words(g, 2, 0, N_TILES)
         warm = keep.tile([P, 2], F32)
         nc.vector.memset(warm[:, 0:1], 0.0)
@@ -135,7 +136,7 @@ def tile_vclinear_w_e_kernel(tc, inputs, W_wts_words, W_wts_scales, b_wts, out):
         for lo in range(2 * DMA_GROUPS, GROUPS, DMA_GROUPS):
             zero_planes(lo)
             load_scales(lo)
-        for g in range(PASSES, GROUPS - PASSES, 2):
+        for g in range(AHEAD * PASSES, GROUPS - PASSES, 2):
             load_words(g, 2, 0, N_TILES)
         for g in range(GROUPS - PASSES, GROUPS, 2):
             load_words(g, 2, 0, 1)

@@ -24,6 +24,7 @@ PASSES = FEATURES // K_PASS
 GROUPS = SDIM * PASSES
 N_TILE = 512
 N_TILES = OUTPUTS // N_TILE
+N_LAST = 128
 WORD_BYTES = 2
 
 RUNS = 1
@@ -158,32 +159,48 @@ def tile_vclinear_w_e_kernel(tc, inputs, W_wts_words, W_wts_scales, b_wts, out):
 
         bias_product()
 
-        for s in range(SDIM):
+        def multiply(dst, s, c, first_col, n_cols):
+            g = PASSES * s + c
+            nc.tensor.matmul_mx(
+                out=dst,
+                lhsT=x_codes[:, c * P : (c + 1) * P].bitcast(FP8X4),
+                lhsT_scale=x_scales[:, c * P : (c + 1) * P],
+                rhs=words[g // 2][:, g % 2, first_col * WORD_BYTES : (first_col + n_cols) * WORD_BYTES].bitcast(FP4X4),
+                rhs_scale=planes[g // DMA_GROUPS][:, g % DMA_GROUPS, first_col : first_col + n_cols],
+                start=(c == 0),
+                stop=(c == PASSES - 1),
+            )
+
+        def add_up(src, s, first_col, n_cols):
+            cols = slice(first_col, first_col + n_cols)
+            nc.vector.scalar_tensor_tensor(
+                out=acc[:, cols],
+                in0=src,
+                scalar=basis[:, s : s + 1],
+                in1=acc[:, cols],
+                op0=ALU.mult,
+                op1=ALU.add,
+            )
+
+        for s in range(SDIM - 1):
             product = [psum.tile([P, N_TILE], F32, tag="bank", name="product%d" % n) for n in range(N_TILES)]
-            if s < SDIM - 1:
-                order = [(c, n) for c in range(PASSES) for n in range(N_TILES)]
-            else:
-                order = [(c, n) for n in range(N_TILES) for c in range(PASSES)]
-            for c, n in order:
-                g = PASSES * s + c
-                nc.tensor.matmul_mx(
-                    out=product[n][:],
-                    lhsT=x_codes[:, c * P : (c + 1) * P].bitcast(FP8X4),
-                    lhsT_scale=x_scales[:, c * P : (c + 1) * P],
-                    rhs=words[g // 2][:, g % 2, n * N_TILE * WORD_BYTES : (n + 1) * N_TILE * WORD_BYTES].bitcast(FP4X4),
-                    rhs_scale=planes[g // DMA_GROUPS][:, g % DMA_GROUPS, n * N_TILE : (n + 1) * N_TILE],
-                    start=(c == 0),
-                    stop=(c == PASSES - 1),
-                )
+            for c in range(PASSES):
+                for n in range(N_TILES):
+                    multiply(product[n][:], s, c, n * N_TILE, N_TILE)
             for n in range(N_TILES):
-                cols = slice(n * N_TILE, (n + 1) * N_TILE)
-                nc.vector.scalar_tensor_tensor(
-                    out=acc[:, cols],
-                    in0=product[n][:],
-                    scalar=basis[:, s : s + 1],
-                    in1=acc[:, cols],
-                    op0=ALU.mult,
-                    op1=ALU.add,
-                )
-                if s == SDIM - 1:
-                    nc.sync.dma_start(out=out[:, cols], in_=acc[:, cols])
+                add_up(product[n][:], s, n * N_TILE, N_TILE)
+
+        s = SDIM - 1
+        first = psum.tile([P, N_TILE], F32, tag="bank")
+        for c in range(PASSES):
+            multiply(first[:], s, c, 0, N_TILE)
+        add_up(first[:], s, 0, N_TILE)
+        nc.sync.dma_start(out=out[:, 0:N_TILE], in_=acc[:, 0:N_TILE])
+        narrow = [psum.tile([P, N_LAST], F32, tag="bank", name="narrow%d" % j) for j in range(N_TILE // N_LAST)]
+        for c in range(PASSES):
+            for j in range(N_TILE // N_LAST):
+                multiply(narrow[j][:], s, c, N_TILE + j * N_LAST, N_LAST)
+        for j in range(N_TILE // N_LAST):
+            lo = N_TILE + j * N_LAST
+            add_up(narrow[j][:], s, lo, N_LAST)
+            nc.sync.dma_start(out=out[:, lo : lo + N_LAST], in_=acc[:, lo : lo + N_LAST])

@@ -45,20 +45,24 @@ def tile_vclinear_w_e_kernel(tc, inputs, W_wts_words, W_wts_scales, b_wts, out):
         x_in = keep.tile([P, FEATURES], BF16, align_bytes=64)
         t_in = keep.tile([P, 2], BF16)
         b_rows = keep.tile([SDIM, OUTPUTS], BF16)
-        words = [
-            keep.tile([P, 2, WORD_BYTES * OUTPUTS], U8, name="words%d" % i, align_bytes=64) for i in range(GROUPS // 2)
-        ]
+        words = {}
         planes = [
-            keep.tile([P, DMA_GROUPS, OUTPUTS], U8, name="planes%d" % lo, align_bytes=64)
+            keep.tile([P, DMA_GROUPS, OUTPUTS], U8, name="planes%d" % lo, align_bytes=256)
             for lo in range(0, GROUPS, DMA_GROUPS)
         ]
 
         def load_words(g, n_groups, first_tile, n_tiles):
             cols = slice(first_tile * N_TILE * WORD_BYTES, (first_tile + n_tiles) * N_TILE * WORD_BYTES)
+            tile = keep.tile(
+                [P, n_groups, n_tiles * N_TILE * WORD_BYTES], U8, name="words%d_%d" % (g, first_tile), align_bytes=256
+            )
             nc.sync.dma_start(
-                out=words[g // 2][:, g % 2 : g % 2 + n_groups, cols].bitcast(I32),
+                out=tile[:].bitcast(I32),
                 in_=W_wts_words[g : g + n_groups, :, cols].rearrange("g p b -> p g b").bitcast(I32),
             )
+            for i in range(n_groups):
+                for n in range(n_tiles):
+                    words[g + i, first_tile + n] = (tile, i, n * N_TILE)
 
         def zero_planes(lo):
             part = planes[lo // DMA_GROUPS][:]
@@ -126,8 +130,8 @@ def tile_vclinear_w_e_kernel(tc, inputs, W_wts_words, W_wts_scales, b_wts, out):
                     )
             nc.scalar.copy(out=grouped_words[:, c0 : c0 + 2, :, :], in_=xt[:].rearrange("p c u b -> p c b u"))
         nc.scalar.copy(out=b_f32[0:SDIM, :], in_=b_rows[:])
-        x_codes = keep.tile([P, PASSES * P], U32, align_bytes=64)
-        x_scales = keep.tile([P, PASSES * P], U8, align_bytes=64)
+        x_codes = keep.tile([P, PASSES * P], U32, align_bytes=256)
+        x_scales = keep.tile([P, PASSES * P], U8, align_bytes=256)
         nc.vector.quantize_mx(
             out=x_codes[:].bitcast(FP8X4),
             scales=x_scales[:],
@@ -161,11 +165,13 @@ def tile_vclinear_w_e_kernel(tc, inputs, W_wts_words, W_wts_scales, b_wts, out):
 
         def multiply(dst, s, c, first_col, n_cols):
             g = PASSES * s + c
+            tile, i, tile_col = words[g, first_col // N_TILE]
+            lo = tile_col + first_col % N_TILE
             nc.tensor.matmul_mx(
                 out=dst,
                 lhsT=x_codes[:, c * P : (c + 1) * P].bitcast(FP8X4),
                 lhsT_scale=x_scales[:, c * P : (c + 1) * P],
-                rhs=words[g // 2][:, g % 2, first_col * WORD_BYTES : (first_col + n_cols) * WORD_BYTES].bitcast(FP4X4),
+                rhs=tile[:, i, lo * WORD_BYTES : (lo + n_cols) * WORD_BYTES].bitcast(FP4X4),
                 rhs_scale=planes[g // DMA_GROUPS][:, g % DMA_GROUPS, first_col : first_col + n_cols],
                 start=(c == 0),
                 stop=(c == PASSES - 1),

@@ -27,9 +27,7 @@ N_TILES = OUTPUTS // N_TILE
 N_LAST = 128
 WORD_BYTES = 2
 
-RUNS = 1
-RUN_GROUPS = GROUPS // RUNS
-DMA_GROUPS = 8
+SCALE_CHUNKS = (8, 18, 6)
 AHEAD = 3
 
 FLOPS = 2 * P * FEATURES * OUTPUTS * SDIM
@@ -46,10 +44,12 @@ def tile_vclinear_w_e_kernel(tc, inputs, W_wts_words, W_wts_scales, b_wts, out):
         t_in = keep.tile([P, 2], BF16)
         b_rows = keep.tile([SDIM, OUTPUTS], BF16)
         words = {}
-        planes = [
-            keep.tile([P, DMA_GROUPS, OUTPUTS], U8, name="planes%d" % lo, align_bytes=256)
-            for lo in range(0, GROUPS, DMA_GROUPS)
-        ]
+        chunks = []
+        plane_of = []
+        for n_groups in SCALE_CHUNKS:
+            tile = keep.tile([P, n_groups, OUTPUTS], U8, name="planes%d" % len(plane_of), align_bytes=256)
+            chunks.append((tile, len(plane_of), n_groups))
+            plane_of.extend((tile, i) for i in range(n_groups))
 
         def load_words(g, n_groups, first_tile, n_tiles):
             cols = slice(first_tile * N_TILE * WORD_BYTES, (first_tile + n_tiles) * N_TILE * WORD_BYTES)
@@ -64,15 +64,14 @@ def tile_vclinear_w_e_kernel(tc, inputs, W_wts_words, W_wts_scales, b_wts, out):
                 for n in range(n_tiles):
                     words[g + i, first_tile + n] = (tile, i, n * N_TILE)
 
-        def zero_planes(lo):
-            part = planes[lo // DMA_GROUPS][:]
-            nc.vector.memset(part.rearrange("p g n -> p (g n)").bitcast(I32), 0)
+        def zero_planes(chunk):
+            nc.vector.memset(chunks[chunk][0][:].rearrange("p g n -> p (g n)").bitcast(I32), 0)
 
-        def load_scales(lo):
-            part = planes[lo // DMA_GROUPS]
+        def load_scales(chunk):
+            part, lo, n_groups = chunks[chunk]
             for j in range(2):
                 for r in range(4):
-                    rows = W_wts_scales[lo : lo + DMA_GROUPS, 4 * j + r : 16 : 8, :]
+                    rows = W_wts_scales[lo : lo + n_groups, 4 * j + r : 16 : 8, :]
                     nc.sync.dma_start(
                         out=part[32 * j + r : P : 64, :, :].bitcast(I32),
                         in_=rows.rearrange("g q n -> q g n").bitcast(I32),
@@ -92,10 +91,10 @@ def tile_vclinear_w_e_kernel(tc, inputs, W_wts_words, W_wts_scales, b_wts, out):
         nc.gpsimd.memset(b_f32[:], 0.0)
         basis = keep.tile([P, P], F32)
         nc.gpsimd.memset(basis[:], 0.0)
-        zero_planes(0)
-        zero_planes(DMA_GROUPS)
-        load_scales(0)
-        load_scales(DMA_GROUPS)
+        for chunk in range(2):
+            zero_planes(chunk)
+        for chunk in range(2):
+            load_scales(chunk)
 
         t = basis[:, 1:2]
         hinge = keep.tile([P, len(KNOTS)], F32)
@@ -138,9 +137,8 @@ def tile_vclinear_w_e_kernel(tc, inputs, W_wts_words, W_wts_scales, b_wts, out):
             in_=grouped[:].rearrange("p c b t -> p (c b t)"),
         )
 
-        for lo in range(2 * DMA_GROUPS, GROUPS, DMA_GROUPS):
-            zero_planes(lo)
-            load_scales(lo)
+        zero_planes(2)
+        load_scales(2)
         for g in range(AHEAD * PASSES, GROUPS - PASSES, 2):
             load_words(g, 2, 0, N_TILES)
         for g in range(GROUPS - PASSES, GROUPS, 2):
@@ -166,13 +164,14 @@ def tile_vclinear_w_e_kernel(tc, inputs, W_wts_words, W_wts_scales, b_wts, out):
         def multiply(dst, s, c, first_col, n_cols):
             g = PASSES * s + c
             tile, i, tile_col = words[g, first_col // N_TILE]
+            plane, k = plane_of[g]
             lo = tile_col + first_col % N_TILE
             nc.tensor.matmul_mx(
                 out=dst,
                 lhsT=x_codes[:, c * P : (c + 1) * P].bitcast(FP8X4),
                 lhsT_scale=x_scales[:, c * P : (c + 1) * P],
                 rhs=tile[:, i, lo * WORD_BYTES : (lo + n_cols) * WORD_BYTES].bitcast(FP4X4),
-                rhs_scale=planes[g // DMA_GROUPS][:, g % DMA_GROUPS, first_col : first_col + n_cols],
+                rhs_scale=plane[:, k, first_col : first_col + n_cols],
                 start=(c == 0),
                 stop=(c == PASSES - 1),
             )

@@ -80,8 +80,7 @@ def tile_vclinear_w_e_kernel(tc, inputs, W_wts_words, W_wts_scales, b_wts, out):
         nc.sync.dma_start(out=x_in[:], in_=inputs[:, 1 : 1 + FEATURES])
         nc.scalar.dma_start(out=t_in[:], in_=inputs[:, 0:2])
         nc.scalar.dma_start(out=b_rows[:], in_=b_wts[:, :])
-        for g in range(0, AHEAD * PASSES, 2):
-            load_words(g, 2, 0, N_TILES)
+        load_words(0, AHEAD * PASSES, 0, N_TILES)
         warm = keep.tile([P, 2], F32)
         nc.vector.memset(warm[:, 0:1], 0.0)
         nc.scalar.copy(out=warm[:, 1:2], in_=warm[:, 0:1])

from contextlib import ExitStack

import concourse.mybir as mybir
from concourse.masks import make_identity

F32 = mybir.dt.float32
BF16 = mybir.dt.bfloat16
I32 = mybir.dt.int32
U32 = mybir.dt.uint32
U8 = mybir.dt.uint8
FP8X4 = mybir.dt.float8_e4m3fn_x4
FP4X4 = mybir.dt.float4_e2m1fn_x4
ALU = mybir.AluOpType

P = 128
FEATURES = 2048
OUTPUTS = 1024
KNOTS = (0.2, 0.4, 0.6, 0.8)
SDIM = 4 + len(KNOTS)

PACK = 4
K_PASS = P * PACK
PASSES = FEATURES // K_PASS
GROUPS = SDIM * PASSES
N_TILE = 512
N_TILES = OUTPUTS // N_TILE
N_LAST = 128
WORD_BYTES = 2

SCALE_CHUNKS = (8, 18, 6)
AHEAD = 3

FLOPS = 2 * P * FEATURES * OUTPUTS * SDIM


def tile_vclinear_w_e_kernel(tc, inputs, W_wts_words, W_wts_scales, b_wts, out):
    nc = tc.nc
    with ExitStack() as ctx:
        ctx.enter_context(tc.manual_schedule())
        keep = ctx.enter_context(tc.tile_pool(name="keep", bufs=1))
        psum = ctx.enter_context(tc.psum_pool(name="psum", bufs=8))

        x_in = keep.tile([P, FEATURES], BF16, align_bytes=64)
        t_in = keep.tile([P, 2], BF16)
        b_rows = keep.tile([SDIM, OUTPUTS], BF16)
        words = {}
        chunks = []
        plane_of = []
        for n_groups in SCALE_CHUNKS:
            tile = keep.tile([P, n_groups, OUTPUTS], U8, name="planes%d" % len(plane_of), align_bytes=256)
            chunks.append((tile, len(plane_of), n_groups))
            plane_of.extend((tile, i) for i in range(n_groups))

        def load_words(g, n_groups, first_tile, n_tiles):
            cols = slice(first_tile * N_TILE * WORD_BYTES, (first_tile + n_tiles) * N_TILE * WORD_BYTES)
            tile = keep.tile(
                [P, n_groups, n_tiles * N_TILE * WORD_BYTES], U8, name="words%d_%d" % (g, first_tile), align_bytes=256
            )
            nc.sync.dma_start(
                out=tile[:].bitcast(I32),
                in_=W_wts_words[g : g + n_groups, :, cols].rearrange("g p b -> p g b").bitcast(I32),
            )
            for i in range(n_groups):
                for n in range(n_tiles):
                    words[g + i, first_tile + n] = (tile, i, n * N_TILE)

        def zero_planes(chunk):
            nc.vector.memset(chunks[chunk][0][:].rearrange("p g n -> p (g n)").bitcast(I32), 0)

        def load_scales(chunk):
            part, lo, n_groups = chunks[chunk]
            for j in range(2):
                for r in range(4):
                    rows = W_wts_scales[lo : lo + n_groups, 4 * j + r : 16 : 8, :]
                    nc.sync.dma_start(
                        out=part[32 * j + r : P : 64, :, :].bitcast(I32),
                        in_=rows.rearrange("g q n -> q g n").bitcast(I32),
                    )

        nc.sync.dma_start(out=x_in[:], in_=inputs[:, 1 : 1 + FEATURES])
        nc.scalar.dma_start(out=t_in[:], in_=inputs[:, 0:2])
        nc.scalar.dma_start(out=b_rows[:], in_=b_wts[:, :])
        load_words(0, AHEAD * PASSES, 0, N_TILES)
        warm = keep.tile([P, 2], F32)
        nc.vector.memset(warm[:, 0:1], 0.0)
        nc.scalar.copy(out=warm[:, 1:2], in_=warm[:, 0:1])
        ident = keep.tile([P, P], F32)
        make_identity(nc, ident[:])
        b_f32 = keep.tile([P, OUTPUTS], F32)
        nc.gpsimd.memset(b_f32[:], 0.0)
        basis = keep.tile([P, P], F32)
        nc.gpsimd.memset(basis[:], 0.0)
        for chunk in range(2):
            zero_planes(chunk)
        for chunk in range(2):
            load_scales(chunk)

        t = basis[:, 1:2]
        hinge = keep.tile([P, len(KNOTS)], F32)
        hinge_sq = keep.tile([P, len(KNOTS)], F32)
        nc.vector.memset(basis[:, 0:1], 1.0)
        nc.vector.tensor_copy(out=t, in_=t_in[:, 0:1])
        nc.vector.tensor_mul(basis[:, 2:3], t, t)
        nc.vector.tensor_mul(basis[:, 3:4], basis[:, 2:3], t)
        for j, knot in enumerate(KNOTS):
            nc.vector.tensor_scalar(
                out=hinge[:, j : j + 1], in0=t, scalar1=knot, scalar2=0.0, op0=ALU.subtract, op1=ALU.max
            )
        nc.vector.tensor_mul(hinge_sq[:], hinge[:], hinge[:])
        nc.vector.tensor_mul(basis[:, 4:SDIM], hinge_sq[:], hinge[:])

        x_words = x_in[:].bitcast(F32)
        grouped = keep.tile([P, PASSES, P, PACK], BF16, align_bytes=64)
        grouped_words = (
            grouped[:]
            .rearrange("p c b t -> p (c b t)")
            .bitcast(F32)
            .rearrange("p (c b u) -> p c b u", c=PASSES, u=2)
        )
        for c0 in range(0, PASSES, 2):
            xt = psum.tile([P, 2, 2, P], F32, tag="bank")
            for c in range(c0, c0 + 2):
                for u in range(2):
                    nc.tensor.transpose(
                        xt[:, c - c0, u, :],
                        x_words[:, 256 * c + u : 256 * (c + 1) : 2],
                        ident[:],
                    )
            nc.scalar.copy(out=grouped_words[:, c0 : c0 + 2, :, :], in_=xt[:].rearrange("p c u b -> p c b u"))
        nc.scalar.copy(out=b_f32[0:SDIM, :], in_=b_rows[:])
        x_codes = keep.tile([P, PASSES * P], U32, align_bytes=256)
        x_scales = keep.tile([P, PASSES * P], U8, align_bytes=256)
        nc.vector.quantize_mx(
            out=x_codes[:].bitcast(FP8X4),
            scales=x_scales[:],
            in_=grouped[:].rearrange("p c b t -> p (c b t)"),
        )

        zero_planes(2)
        load_scales(2)
        for g in range(AHEAD * PASSES, GROUPS - PASSES, 2):
            load_words(g, 2, 0, N_TILES)
        for g in range(GROUPS - PASSES, GROUPS, 2):
            load_words(g, 2, 0, 1)
        for g in range(GROUPS - PASSES, GROUPS):
            load_words(g, 1, 1, 1)

        acc = keep.tile([P, OUTPUTS], F32)

        def bias_product():
            basis_t_ps = psum.tile([P, P], F32, tag="bank")
            nc.tensor.transpose(basis_t_ps[:], basis[:], ident[:])
            basis_t = keep.tile([P, P], F32)
            nc.scalar.copy(out=basis_t[:], in_=basis_t_ps[:])
            for n in range(N_TILES):
                cols = slice(n * N_TILE, (n + 1) * N_TILE)
                bias_ps = psum.tile([P, N_TILE], F32, tag="bank")
                nc.tensor.matmul(out=bias_ps[:], lhsT=basis_t[:], rhs=b_f32[:, cols], start=True, stop=True)
                nc.scalar.copy(out=acc[:, cols], in_=bias_ps[:])

        bias_product()

        def multiply(dst, s, c, first_col, n_cols):
            g = PASSES * s + c
            tile, i, tile_col = words[g, first_col // N_TILE]
            plane, k = plane_of[g]
            lo = tile_col + first_col % N_TILE
            nc.tensor.matmul_mx(
                out=dst,
                lhsT=x_codes[:, c * P : (c + 1) * P].bitcast(FP8X4),
                lhsT_scale=x_scales[:, c * P : (c + 1) * P],
                rhs=tile[:, i, lo * WORD_BYTES : (lo + n_cols) * WORD_BYTES].bitcast(FP4X4),
                rhs_scale=plane[:, k, first_col : first_col + n_cols],
                start=(c == 0),
                stop=(c == PASSES - 1),
            )

        def add_up(src, s, first_col, n_cols):
            cols = slice(first_col, first_col + n_cols)
            nc.vector.scalar_tensor_tensor(
                out=acc[:, cols],
                in0=src,
                scalar=basis[:, s : s + 1],
                in1=acc[:, cols],
                op0=ALU.mult,
                op1=ALU.add,
            )

        for s in range(SDIM - 1):
            product = [psum.tile([P, N_TILE], F32, tag="bank", name="product%d" % n) for n in range(N_TILES)]
            for c in range(PASSES):
                for n in range(N_TILES):
                    multiply(product[n][:], s, c, n * N_TILE, N_TILE)
            for n in range(N_TILES):
                add_up(product[n][:], s, n * N_TILE, N_TILE)

        s = SDIM - 1
        first = psum.tile([P, N_TILE], F32, tag="bank")
        for c in range(PASSES):
            multiply(first[:], s, c, 0, N_TILE)
        add_up(first[:], s, 0, N_TILE)
        nc.sync.dma_start(out=out[:, 0:N_TILE], in_=acc[:, 0:N_TILE])
        narrow = [psum.tile([P, N_LAST], F32, tag="bank", name="narrow%d" % j) for j in range(N_TILE // N_LAST)]
        for c in range(PASSES):
            for j in range(N_TILE // N_LAST):
                multiply(narrow[j][:], s, c, N_TILE + j * N_LAST, N_LAST)
        for j in range(N_TILE // N_LAST):
            lo = N_TILE + j * N_LAST
            add_up(narrow[j][:], s, lo, N_LAST)
            nc.sync.dma_start(out=out[:, lo : lo + N_LAST], in_=acc[:, lo : lo + N_LAST])
